import numpy as np
import ml_dtypes

BF16 = ml_dtypes.bfloat16


def bf(x):
    return np.asarray(x, np.float32).astype(BF16)


def f32(x):
    return np.asarray(x, np.float32)


def f64(x):
    return np.asarray(x).astype(np.float64)


def striped(idx):
    return np.tile(idx.reshape(-1, 16).T, (8, 1))


D, S, R, K, E, N = 128, 256, 128, 4, 256, 512


def setup_inputs():
    return {
        "table": bf(np.random.standard_normal((D, S))),
        "w_src": bf(np.random.standard_normal((D, D)) / np.sqrt(2.0 * D)),
        "w_tgt": bf(np.random.standard_normal((D, D)) / np.sqrt(2.0 * D)),
        "b": f32(0.2 * np.random.standard_normal((D, 1))),
        "offs": striped(np.concatenate([np.random.permutation(S)[:R] for _ in range(K)])),
    }


def reference(table, w_src, w_tgt, b, offs):
    idx = offs[:16].T.reshape(-1)
    t = f64(table)
    src = t[:, idx[:E]]
    tgt = t[:, idx[E:]]
    h = np.tanh(f64(w_src).T @ src + f64(w_tgt).T @ tgt + f64(b))
    mid = 0.5 * (src + tgt)
    return np.concatenate([h, mid], axis=0)

@@ -1,0 +1,60 @@
+import concourse.mybir as mybir
+
+BF16, F32, U16 = mybir.dt.bfloat16, mybir.dt.float32, mybir.dt.uint16
+
+D = 128
+S = 256
+E = 256
+N = 2 * E
+COLS = E // 16
+
+FLOPS = 2 * (2 * D * D * E)
+
+
+def tile_hierarchicalpooling_kernel(tc, table, w_src, w_tgt, b, offs, out):
+    nc = tc.nc
+    with (
+        tc.tile_pool(name="held", bufs=1) as held,
+        tc.psum_pool(name="psum", bufs=1) as psum,
+    ):
+        offsets = held.tile([D, N // 16], U16, name="offsets")
+        nc.sync.dma_start(offsets[:], offs)
+        nodes = held.tile([D, S], BF16, name="nodes")
+        nc.sync.dma_start(nodes[:], table)
+        src_weights = held.tile([D, D], BF16, name="src_weights")
+        nc.sync.dma_start(src_weights[:], w_src)
+        tgt_weights = held.tile([D, D], BF16, name="tgt_weights")
+        nc.sync.dma_start(tgt_weights[:], w_tgt)
+        bias = held.tile([D, 1], F32, name="bias")
+        nc.sync.dma_start(bias[:], b)
+
+        half_identity = held.tile([D, D], BF16, name="half_identity")
+        nc.gpsimd.memset(half_identity[:], 0.0)
+        nc.gpsimd.affine_select(
+            out=half_identity[:],
+            in_=half_identity[:],
+            pattern=[[-1, D]],
+            compare_op=mybir.AluOpType.not_equal,
+            fill=0.5,
+            base=0,
+            channel_multiplier=1,
+        )
+
+        src_nodes = nodes[:].indirect(offsets[:, 0:COLS])
+        tgt_nodes = nodes[:].indirect(offsets[:, COLS : 2 * COLS])
+
+        projected = psum.tile([D, E], F32, name="projected")
+        nc.tensor.matmul(projected[:], src_weights[:], src_nodes, start=True, stop=False)
+        nc.tensor.matmul(projected[:], tgt_weights[:], tgt_nodes, start=False, stop=True)
+        hidden = held.tile([D, E], F32, name="hidden")
+        nc.scalar.activation(
+            hidden[:], projected[:], mybir.ActivationFunctionType.Tanh, bias=bias[:]
+        )
+        nc.sync.dma_start(out[0:D, :], hidden[:])
+
+        averaged = psum.tile([D, E], F32, name="averaged")
+        nc.tensor.matmul(averaged[:], half_identity[:], src_nodes, start=True, stop=False)
+        nc.tensor.matmul(averaged[:], half_identity[:], tgt_nodes, start=False, stop=True)
+        mid = held.tile([D, E], F32, name="mid")
+        nc.vector.tensor_copy(mid[:], averaged[:])
+        nc.sync.dma_start(out[D : 2 * D, :], mid[:])

@@ -20,13 +20,13 @@ def tile_hierarchicalpooling_kernel(tc, table, w_src, w_tgt, b, offs, out):
         offsets = held.tile([D, N // 16], U16, name="offsets")
         nc.sync.dma_start(offsets[:], offs)
         nodes = held.tile([D, S], BF16, name="nodes")
-        nc.sync.dma_start(nodes[:], table)
+        nc.scalar.dma_start(nodes[:], table)
         src_weights = held.tile([D, D], BF16, name="src_weights")
         nc.sync.dma_start(src_weights[:], w_src)
         tgt_weights = held.tile([D, D], BF16, name="tgt_weights")
-        nc.sync.dma_start(tgt_weights[:], w_tgt)
+        nc.scalar.dma_start(tgt_weights[:], w_tgt)
         bias = held.tile([D, 1], F32, name="bias")
-        nc.sync.dma_start(bias[:], b)
+        nc.gpsimd.dma_start(bias[:], b)
 
         half_identity = held.tile([D, D], BF16, name="half_identity")
         nc.gpsimd.memset(half_identity[:], 0.0)

@@ -28,6 +28,10 @@ def tile_hierarchicalpooling_kernel(tc, table, w_src, w_tgt, b, offs, out):
         bias = held.tile([D, 1], F32, name="bias")
         nc.gpsimd.dma_start(bias[:], b)
 
+        early = held.tile([D, 1], F32, name="early")
+        nc.vector.memset(early[:], 0.0)
+        nc.scalar.activation(early[:], early[:], mybir.ActivationFunctionType.Tanh)
+
         half_identity = held.tile([D, D], BF16, name="half_identity")
         nc.gpsimd.memset(half_identity[:], 0.0)
         nc.gpsimd.affine_select(

@@ -26,7 +26,7 @@ def tile_hierarchicalpooling_kernel(tc, table, w_src, w_tgt, b, offs, out):
         tgt_weights = held.tile([D, D], BF16, name="tgt_weights")
         nc.scalar.dma_start(tgt_weights[:], w_tgt)
         bias = held.tile([D, 1], F32, name="bias")
-        nc.gpsimd.dma_start(bias[:], b)
+        nc.sync.dma_start(bias[:], b)
 
         early = held.tile([D, 1], F32, name="early")
         nc.vector.memset(early[:], 0.0)

@@ -7,6 +7,7 @@ S = 256
 E = 256
 N = 2 * E
 COLS = E // 16
+LAST = 64
 
 FLOPS = 2 * (2 * D * D * E)
 
@@ -44,21 +45,34 @@ def tile_hierarchicalpooling_kernel(tc, table, w_src, w_tgt, b, offs, out):
             channel_multiplier=1,
         )
 
-        src_nodes = nodes[:].indirect(offsets[:, 0:COLS])
-        tgt_nodes = nodes[:].indirect(offsets[:, COLS : 2 * COLS])
-
         projected = psum.tile([D, E], F32, name="projected")
-        nc.tensor.matmul(projected[:], src_weights[:], src_nodes, start=True, stop=False)
-        nc.tensor.matmul(projected[:], tgt_weights[:], tgt_nodes, start=False, stop=True)
+        nc.tensor.matmul(
+            projected[:], src_weights[:], nodes[:].indirect(offsets[:, 0:COLS]),
+            start=True, stop=False,
+        )
+        nc.tensor.matmul(
+            projected[:], tgt_weights[:], nodes[:].indirect(offsets[:, COLS : 2 * COLS]),
+            start=False, stop=True,
+        )
         hidden = held.tile([D, E], F32, name="hidden")
         nc.scalar.activation(
             hidden[:], projected[:], mybir.ActivationFunctionType.Tanh, bias=bias[:]
         )
         nc.sync.dma_start(out[0:D, :], hidden[:])
 
-        averaged = psum.tile([D, E], F32, name="averaged")
-        nc.tensor.matmul(averaged[:], half_identity[:], src_nodes, start=True, stop=False)
-        nc.tensor.matmul(averaged[:], half_identity[:], tgt_nodes, start=False, stop=True)
-        mid = held.tile([D, E], F32, name="mid")
-        nc.vector.tensor_copy(mid[:], averaged[:])
-        nc.sync.dma_start(out[D : 2 * D, :], mid[:])
+        for first, last in ((0, E - LAST), (E - LAST, E)):
+            width = last - first
+            averaged = psum.tile([D, width], F32, name="averaged%d" % first)
+            nc.tensor.matmul(
+                averaged[:], half_identity[:],
+                nodes[:].indirect(offsets[:, first // 16 : last // 16]),
+                start=True, stop=False,
+            )
+            nc.tensor.matmul(
+                averaged[:], half_identity[:],
+                nodes[:].indirect(offsets[:, COLS + first // 16 : COLS + last // 16]),
+                start=False, stop=True,
+            )
+            mid = held.tile([D, width], F32, name="mid%d" % first)
+            nc.vector.tensor_copy(mid[:], averaged[:])
+            nc.sync.dma_start(out[D : 2 * D, first:last], mid[:])

@@ -7,7 +7,7 @@ S = 256
 E = 256
 N = 2 * E
 COLS = E // 16
-LAST = 64
+LAST = 128
 
 FLOPS = 2 * (2 * D * D * E)
 

@@ -18,12 +18,12 @@ def tile_hierarchicalpooling_kernel(tc, table, w_src, w_tgt, b, offs, out):
         tc.tile_pool(name="held", bufs=1) as held,
         tc.psum_pool(name="psum", bufs=1) as psum,
     ):
-        offsets = held.tile([D, N // 16], U16, name="offsets")
-        nc.sync.dma_start(offsets[:], offs)
-        nodes = held.tile([D, S], BF16, name="nodes")
-        nc.scalar.dma_start(nodes[:], table)
         src_weights = held.tile([D, D], BF16, name="src_weights")
         nc.sync.dma_start(src_weights[:], w_src)
+        nodes = held.tile([D, S], BF16, name="nodes")
+        nc.scalar.dma_start(nodes[:], table)
+        offsets = held.tile([D, N // 16], U16, name="offsets")
+        nc.sync.dma_start(offsets[:], offs)
         tgt_weights = held.tile([D, D], BF16, name="tgt_weights")
         nc.scalar.dma_start(tgt_weights[:], w_tgt)
         bias = held.tile([D, 1], F32, name="bias")

@@ -18,10 +18,10 @@ def tile_hierarchicalpooling_kernel(tc, table, w_src, w_tgt, b, offs, out):
         tc.tile_pool(name="held", bufs=1) as held,
         tc.psum_pool(name="psum", bufs=1) as psum,
     ):
-        src_weights = held.tile([D, D], BF16, name="src_weights")
-        nc.sync.dma_start(src_weights[:], w_src)
         nodes = held.tile([D, S], BF16, name="nodes")
-        nc.scalar.dma_start(nodes[:], table)
+        nc.sync.dma_start(nodes[:], table)
+        src_weights = held.tile([D, D], BF16, name="src_weights")
+        nc.scalar.dma_start(src_weights[:], w_src)
         offsets = held.tile([D, N // 16], U16, name="offsets")
         nc.sync.dma_start(offsets[:], offs)
         tgt_weights = held.tile([D, D], BF16, name="tgt_weights")

@@ -7,7 +7,7 @@ S = 256
 E = 256
 N = 2 * E
 COLS = E // 16
-LAST = 128
+PIECE = E // 2
 
 FLOPS = 2 * (2 * D * D * E)
 
@@ -60,19 +60,17 @@ def tile_hierarchicalpooling_kernel(tc, table, w_src, w_tgt, b, offs, out):
         )
         nc.sync.dma_start(out[0:D, :], hidden[:])
 
-        for first, last in ((0, E - LAST), (E - LAST, E)):
-            width = last - first
-            averaged = psum.tile([D, width], F32, name="averaged%d" % first)
-            nc.tensor.matmul(
-                averaged[:], half_identity[:],
-                nodes[:].indirect(offsets[:, first // 16 : last // 16]),
-                start=True, stop=False,
-            )
-            nc.tensor.matmul(
-                averaged[:], half_identity[:],
-                nodes[:].indirect(offsets[:, COLS + first // 16 : COLS + last // 16]),
-                start=False, stop=True,
-            )
-            mid = held.tile([D, width], F32, name="mid%d" % first)
-            nc.vector.tensor_copy(mid[:], averaged[:])
-            nc.sync.dma_start(out[D : 2 * D, first:last], mid[:])
+        averaged = psum.tile([D, E], F32, name="averaged")
+        nc.tensor.matmul(
+            averaged[:], half_identity[:], nodes[:].indirect(offsets[:, 0:COLS]),
+            start=True, stop=False,
+        )
+        nc.tensor.matmul(
+            averaged[:], half_identity[:], nodes[:].indirect(offsets[:, COLS : 2 * COLS]),
+            start=False, stop=True,
+        )
+        for first in range(0, E, PIECE):
+            piece = slice(first, first + PIECE)
+            mid = held.tile([D, PIECE], F32, name="mid%d" % first)
+            nc.vector.tensor_copy(mid[:], averaged[:, piece])
+            nc.sync.dma_start(out[D : 2 * D, piece], mid[:])

import concourse.mybir as mybir

BF16, F32, U16 = mybir.dt.bfloat16, mybir.dt.float32, mybir.dt.uint16

D = 128
S = 256
E = 256
N = 2 * E
COLS = E // 16
PIECE = E // 2

FLOPS = 2 * (2 * D * D * E)


def tile_hierarchicalpooling_kernel(tc, table, w_src, w_tgt, b, offs, out):
    nc = tc.nc
    with (
        tc.tile_pool(name="held", bufs=1) as held,
        tc.psum_pool(name="psum", bufs=1) as psum,
    ):
        nodes = held.tile([D, S], BF16, name="nodes")
        nc.sync.dma_start(nodes[:], table)
        src_weights = held.tile([D, D], BF16, name="src_weights")
        nc.scalar.dma_start(src_weights[:], w_src)
        offsets = held.tile([D, N // 16], U16, name="offsets")
        nc.sync.dma_start(offsets[:], offs)
        tgt_weights = held.tile([D, D], BF16, name="tgt_weights")
        nc.scalar.dma_start(tgt_weights[:], w_tgt)
        bias = held.tile([D, 1], F32, name="bias")
        nc.sync.dma_start(bias[:], b)

        early = held.tile([D, 1], F32, name="early")
        nc.vector.memset(early[:], 0.0)
        nc.scalar.activation(early[:], early[:], mybir.ActivationFunctionType.Tanh)

        half_identity = held.tile([D, D], BF16, name="half_identity")
        nc.gpsimd.memset(half_identity[:], 0.0)
        nc.gpsimd.affine_select(
            out=half_identity[:],
            in_=half_identity[:],
            pattern=[[-1, D]],
            compare_op=mybir.AluOpType.not_equal,
            fill=0.5,
            base=0,
            channel_multiplier=1,
        )

        projected = psum.tile([D, E], F32, name="projected")
        nc.tensor.matmul(
            projected[:], src_weights[:], nodes[:].indirect(offsets[:, 0:COLS]),
            start=True, stop=False,
        )
        nc.tensor.matmul(
            projected[:], tgt_weights[:], nodes[:].indirect(offsets[:, COLS : 2 * COLS]),
            start=False, stop=True,
        )
        hidden = held.tile([D, E], F32, name="hidden")
        nc.scalar.activation(
            hidden[:], projected[:], mybir.ActivationFunctionType.Tanh, bias=bias[:]
        )
        nc.sync.dma_start(out[0:D, :], hidden[:])

        averaged = psum.tile([D, E], F32, name="averaged")
        nc.tensor.matmul(
            averaged[:], half_identity[:], nodes[:].indirect(offsets[:, 0:COLS]),
            start=True, stop=False,
        )
        nc.tensor.matmul(
            averaged[:], half_identity[:], nodes[:].indirect(offsets[:, COLS : 2 * COLS]),
            start=False, stop=True,
        )
        for first in range(0, E, PIECE):
            piece = slice(first, first + PIECE)
            mid = held.tile([D, PIECE], F32, name="mid%d" % first)
            nc.vector.tensor_copy(mid[:], averaged[:, piece])
            nc.sync.dma_start(out[D : 2 * D, piece], mid[:])
